import numpy as np
import ml_dtypes


def mxq(x, axis, fmt="e4m3"):
    dtype, down = {"e4m3": (ml_dtypes.float8_e4m3fn, 7), "e5m2": (ml_dtypes.float8_e5m2, 14)}[fmt]
    v = np.moveaxis(np.asarray(x, np.float32).astype(ml_dtypes.bfloat16).astype(np.float64), axis, -1)
    blocks = v.reshape(v.shape[:-1] + (-1, 32))
    amax = np.abs(blocks).max(-1, keepdims=True)
    byte = np.maximum(np.where(amax > 0, np.frexp(amax)[1] - 1 + 127, 0) - down, 1)
    scale = np.exp2(byte - 127.0)
    codes = (blocks / scale).astype(np.float32).astype(dtype).astype(np.float64)
    return np.moveaxis((codes * scale).reshape(v.shape), -1, axis)


WIDE = False


def mx_kscale(k):
    if not WIDE:
        return np.ones(k)
    levels = np.array([10, -10, 5, -5, 0])
    a = np.random.permutation(np.resize(levels, k // 512 * 4)).reshape(k // 512, 4)
    idx = np.arange(k)
    return np.exp2(a[idx // 512, idx % 128 // 32])


BF16 = ml_dtypes.bfloat16


def bf(x):
    return np.asarray(x, np.float32).astype(BF16)


def f64(x):
    return np.asarray(x).astype(np.float64)


B, IN_F, OUT_F = 4096, 2048, 512
IN_Q = IN_F // 4
OUT_Q = OUT_F // 4


def setup_inputs():
    s = mx_kscale(IN_Q)
    scale = 1.0 / np.sqrt(IN_Q)
    inp = {"x": bf((np.random.standard_normal((B, 4, IN_Q)) * s).reshape(B, IN_F))}
    for name in ["rr", "ri", "rj", "rk"]:
        inp["W_" + name] = bf(np.random.uniform(-scale, scale, (OUT_Q, IN_Q)) / s[None, :])
    for name in ["rr", "ri", "rj", "rk"]:
        inp["b_" + name] = bf(np.random.standard_normal(OUT_Q) * 0.5)
    return inp


def reference(x, W_rr, W_ri, W_rj, W_rk, b_rr, b_ri, b_rj, b_rk):
    b = x.shape[0]
    xs = f64(x).reshape(b, 4, IN_Q)
    W = np.stack([f64(W_rr), f64(W_ri), f64(W_rj), f64(W_rk)])
    bias = np.stack([f64(b_rr), f64(b_ri), f64(b_rj), f64(b_rk)])
    xq = mxq(xs, 2, "e4m3")
    Wq = mxq(W, 2, "e4m3")
    Y = (xq.reshape(b * 4, IN_Q) @ Wq.reshape(4 * OUT_Q, IN_Q).T).reshape(b, 4, 4, OUT_Q) + bias
    out_r = Y[:, 0, 0] - Y[:, 1, 1] - Y[:, 2, 2] - Y[:, 3, 3]
    out_i = Y[:, 0, 1] + Y[:, 1, 0] + Y[:, 2, 3] - Y[:, 3, 2]
    out_j = Y[:, 0, 2] - Y[:, 1, 3] + Y[:, 2, 0] + Y[:, 3, 1]
    out_k = Y[:, 0, 3] + Y[:, 1, 2] - Y[:, 2, 1] + Y[:, 3, 0]
    out = np.stack([out_r, out_i, out_j, out_k], axis=1)
    return out.reshape(b, -1)

from contextlib import ExitStack

import concourse.mybir as mybir
from concourse.masks import make_identity

F32 = mybir.dt.float32
BF16 = mybir.dt.bfloat16
U32 = mybir.dt.uint32
U8 = mybir.dt.uint8
I32 = mybir.dt.int32
FP8X4 = mybir.dt.float8_e4m3fn_x4
ADD = mybir.AluOpType.add
MULT = mybir.AluOpType.mult

P = 128
TILES = 32
FLOPS = 2 * 16384 * 512 * 512

GROUPS = [[2 * g, 2 * g + 1] for g in range(16)]
LOADS = [(0, 1), (1, 1)] + [(2 * g, 2) for g in range(1, 16)]
LOADS_AHEAD = 9


def tile_qdense_t_kernel(tc, x, W_rr, W_ri, W_rj, W_rk, b_rr, b_ri, b_rj, b_rk, out):
    nc = tc.nc
    weights = [W_rr, W_ri, W_rj, W_rk]
    biases = [b_rr, b_ri, b_rj, b_rk]
    x_rows = x.rearrange("(p t) k -> p t k", t=TILES)
    out_rows = out.rearrange("(p t) n -> p t n", t=TILES)

    with ExitStack() as ctx:
        const = ctx.enter_context(tc.tile_pool(name="const", bufs=1))
        xpool = ctx.enter_context(tc.tile_pool(name="xres", bufs=1))
        gpool = ctx.enter_context(tc.tile_pool(name="grouped", bufs=4))
        qpool = ctx.enter_context(tc.tile_pool(name="codes", bufs=8))
        opool = ctx.enter_context(tc.tile_pool(name="outs", bufs=6))
        psum = ctx.enter_context(tc.psum_pool(name="psum", bufs=1))
        ctx.enter_context(tc.manual_schedule())

        banks_used = [0]

        def new_bank():
            b = banks_used[0] % 8
            banks_used[0] += 1
            return psum.tile([P, 512], F32, name="bank%d" % b, tag="bank%d" % b)

        ident = const.tile([P, P], F32, name="ident")
        make_identity(nc, ident[:])
        q_scales = const.tile([P, 1024], U8, name="q_scales", align_bytes=64)
        nc.vector.memset(q_scales[:].bitcast(I32), 0)
        b_rows = const.tile([P, P], BF16, name="b_rows")
        nc.vector.memset(b_rows[:], 0.0)
        ones = const.tile([P, P], BF16, name="ones")
        nc.vector.memset(ones[:], 1.0)
        signs = const.tile([P, 4, P], BF16, name="signs")
        nc.vector.memset(signs[:], 1.0)
        nc.vector.memset(signs[32:64, 0, :], -1.0)
        nc.vector.memset(signs[64:128, 0, :], -1.0)
        nc.vector.memset(signs[64:96, 1, :], -1.0)
        nc.vector.memset(signs[96:128, 2, :], -1.0)
        nc.vector.memset(signs[32:64, 3, :], -1.0)

        w_sb = const.tile([P, 2048], BF16, name="w_sb")
        for q in range(4):
            nc.sync.dma_start(out=w_sb[:, 512 * q:512 * (q + 1)], in_=weights[q])
        for q in range(4):
            nc.scalar.dma_start(out=b_rows[32 * q:32 * q + 1, :],
                                in_=biases[q].rearrange("(o n) -> o n", o=1))

        x_words = {}

        def load(i):
            t0, nt = LOADS[i]
            xs = xpool.tile([P, nt * 2048], BF16, name="x%d" % t0)
            nc.sync.dma_start(out=xs[:].rearrange("p (t k) -> p t k", t=nt),
                              in_=x_rows[:, t0:t0 + nt, :])
            words = xs[:].bitcast(F32)
            for j in range(nt):
                x_words[t0 + j] = words[:, 1024 * j:1024 * (j + 1)]

        for i in range(LOADS_AHEAD):
            load(i)

        def flip(words):
            got = []
            for h in range(2):
                bank = new_bank()
                for s in range(4):
                    nc.tensor.transpose(bank[:, P * s:P * (s + 1)],
                                        words[:, 512 * h + P * s:512 * h + P * (s + 1)],
                                        ident[:])
                got.append(bank)
            return got

        def regroup(engine_copy, bank, dst_words):
            engine_copy(out=dst_words.rearrange("p (c r u) -> p c r u", c=2, u=2),
                        in_=bank[:].rearrange("p (c u r) -> p c r u", c=2, u=2))

        w_banks = flip(w_sb[:].bitcast(F32))
        w_pn = const.tile([P, 4096], BF16, name="w_pn", align_bytes=64)
        w_pn_words = w_pn[:].bitcast(F32)
        regroup(nc.scalar.copy, w_banks[0], w_pn_words[:, 0:512])

        b_signed = const.tile([P, 4, P], BF16, name="b_signed")
        nc.vector.tensor_tensor(out=b_signed[:], in0=signs[:],
                                in1=b_rows[:].unsqueeze(1).to_broadcast([P, 4, P]), op=MULT)
        regroup(nc.vector.tensor_copy, w_banks[1], w_pn_words[:, 512:1024])

        bias_ps = new_bank()
        nc.tensor.matmul(bias_ps[:], lhsT=ones[:], rhs=b_signed[:].rearrange("p o n -> p (o n)"),
                         start=True, stop=True)
        bias_bc = const.tile([P, 512], F32, name="bias_bc")
        nc.scalar.copy(out=bias_bc[:], in_=bias_ps[:])

        q_codes = const.tile([P, 1024], U32, name="q_codes", align_bytes=64)
        nc.vector.quantize_mx(out=q_codes[:, 0:512].bitcast(FP8X4), scales=q_scales[:, 0:512],
                              in_=w_pn[:, 0:2048])
        pos = w_pn[:, 0:2048].rearrange("p (q e) -> p q e", q=4)
        neg = w_pn[:, 2048:4096].rearrange("p (q e) -> p q e", q=4)
        nc.vector.tensor_scalar_mul(out=neg[:, 0:2, :], in0=pos[:, 1:4:2, :], scalar1=-1.0)
        nc.vector.tensor_scalar_mul(out=neg[:, 2:4, :], in0=pos[:, 2:4, :], scalar1=-1.0)
        nc.vector.quantize_mx(out=q_codes[:, 512:1024].bitcast(FP8X4), scales=q_scales[:, 512:1024],
                              in_=w_pn[:, 2048:4096])

        r_codes = const.tile([P, 1536], U32, name="r_codes", align_bytes=64)
        r_scales = const.tile([P, 1536], U8, name="r_scales", align_bytes=64)
        views = [
            (r_codes[:].bitcast(I32).rearrange("p (d w) -> p d w", d=12),
             q_codes[:].bitcast(I32).rearrange("p (d w) -> p d w", d=8)),
            (r_scales[:].bitcast(I32).rearrange("p (d w) -> p d w", d=12),
             q_scales[:].bitcast(I32).rearrange("p (d w) -> p d w", d=8)),
        ]

        def move(dst, src):
            for r_v, q_v in views:
                nc.vector.tensor_copy(out=r_v[:, dst, :], in_=q_v[:, src, :])

        rhs = [(q_codes[:, 0:512], q_scales[:, 0:512])]
        for c in range(3):
            rhs.append((r_codes[:, 512 * c:512 * (c + 1)], r_scales[:, 512 * c:512 * (c + 1)]))

        t_banks = {}
        grouped = {}
        packed = {}

        def stage_t(g):
            for t in GROUPS[g]:
                t_banks[t] = flip(x_words[t])

        def stage_c(g):
            for t in GROUPS[g]:
                gr = gpool.tile([P, 2048], BF16, name="grouped", tag="grouped", align_bytes=64)
                gw = gr[:].bitcast(F32)
                for h in range(2):
                    regroup(nc.scalar.copy, t_banks[t][h], gw[:, 512 * h:512 * (h + 1)])
                grouped[t] = gr

        def stage_q(t):
            codes = qpool.tile([P, 512], U32, name="codes", tag="codes", align_bytes=64)
            scales = qpool.tile([P, 512], U8, name="scales", tag="scales", align_bytes=64)
            nc.vector.quantize_mx(out=codes[:].bitcast(FP8X4), scales=scales[:], in_=grouped[t][:])
            packed[t] = (codes, scales)

        accs = {}

        def stage_m(g):
            for t in GROUPS[g]:
                acc = new_bank()
                codes, scales = packed[t]
                for c in range(4):
                    nc.tensor.matmul_mx(out=acc[:],
                                        lhsT=codes[:, P * c:P * (c + 1)].bitcast(FP8X4),
                                        lhsT_scale=scales[:, P * c:P * (c + 1)],
                                        rhs=rhs[c][0].bitcast(FP8X4),
                                        rhs_scale=rhs[c][1],
                                        start=(c == 0), stop=(c == 3))
                accs[t] = acc

        stage_t(0)
        stage_c(0)
        move(slice(0, 5, 2), slice(4, 7))
        move(slice(1, 4, 2), slice(0, 3, 2))
        stage_q(GROUPS[0][0])
        move(slice(7, 10), slice(4, 7))
        move(slice(6, 11, 4), slice(0, 2))
        move(slice(5, 6), slice(3, 4))
        move(slice(11, 12), slice(0, 1))
        stage_q(GROUPS[0][1])

        next_load = LOADS_AHEAD
        n_groups = len(GROUPS)
        for g in range(n_groups):
            last = g == n_groups - 1
            if not last:
                stage_t(g + 1)
                stage_c(g + 1)
            stage_m(g)
            tiles = GROUPS[g]
            ot = opool.tile([P, len(tiles), 512], F32, name="ot", tag="ot")
            for j, t in enumerate(tiles):
                if not last:
                    stage_q(GROUPS[g + 1][j])
                nc.vector.tensor_tensor(out=ot[:, j, :], in0=accs[t][:], in1=bias_bc[:], op=ADD)
                if last:
                    nc.sync.dma_start(out=out_rows[:, t:t + 1, :], in_=ot[:, j:j + 1, :])
            if not last:
                nc.sync.dma_start(out=out_rows[:, tiles[0]:tiles[0] + len(tiles), :], in_=ot[:])
            if next_load < len(LOADS):
                load(next_load)
                next_load += 1
